import numpy as np
import ml_dtypes


def mxq(x, axis, fmt="e4m3"):
    dtype, down = {"e4m3": (ml_dtypes.float8_e4m3fn, 7), "e5m2": (ml_dtypes.float8_e5m2, 14)}[fmt]
    v = np.moveaxis(np.asarray(x, np.float32).astype(ml_dtypes.bfloat16).astype(np.float64), axis, -1)
    blocks = v.reshape(v.shape[:-1] + (-1, 32))
    amax = np.abs(blocks).max(-1, keepdims=True)
    byte = np.maximum(np.where(amax > 0, np.frexp(amax)[1] - 1 + 127, 0) - down, 1)
    scale = np.exp2(byte - 127.0)
    codes = (blocks / scale).astype(np.float32).astype(dtype).astype(np.float64)
    return np.moveaxis((codes * scale).reshape(v.shape), -1, axis)


WIDE = False


def mx_kscale(k):
    if not WIDE:
        return np.ones(k)
    levels = np.array([30, -30])
    if k % 512:
        return np.exp2(np.random.permutation(np.resize(levels, k // 32))).repeat(32)
    a = np.empty((k // 512, 16))
    for p in range(k // 512):
        a[p, :8] = np.random.permutation(np.resize(levels, 8))
        for g in range(8):
            far = levels[np.abs(levels - a[p, g]) >= 10]
            a[p, g + 8] = far[np.random.randint(len(far))]
    return np.exp2(a.ravel()).repeat(32)


BF16 = ml_dtypes.bfloat16


def bf(x):
    return np.asarray(x, np.float32).astype(BF16)


def f64(x):
    return np.asarray(x).astype(np.float64)


E2M1 = np.array([0.0, 0.5, 1.0, 1.5, 2.0, 3.0, 4.0, 6.0, -0.0, -0.5, -1.0, -1.5, -2.0, -3.0, -4.0, -6.0])


def pack_weight(w, fmt):
    k, n = w.shape
    w = f64(bf(w)).reshape(k // 32, 32, n)
    amax = np.abs(w).max(1)
    if fmt == "e4m3":
        byte = np.frexp(amax)[1] - 1 + 127 - 7
    else:
        mant, ex = np.frexp(amax / 6.0)
        byte = np.where(mant > 0.5, ex, ex - 1) + 127
    byte = np.clip(np.where(amax > 0, byte, 1), 1, 254)
    scaled = (w * np.exp2(127.0 - byte)[:, None, :]).reshape(k, n).astype(np.float32)
    by_word = np.ascontiguousarray(scaled.reshape(k // 512, 128, 4, n).transpose(0, 1, 3, 2))
    if fmt == "e4m3":
        words = by_word.astype(ml_dtypes.float8_e4m3fn).view(np.uint8)
    else:
        c = by_word.astype(ml_dtypes.float4_e2m1fn).view(np.uint8) & 0xF
        words = c[..., 0::2] | (c[..., 1::2] << 4)
    return np.ascontiguousarray(words), np.ascontiguousarray(byte.astype(np.uint8).reshape(k // 512, 16, n))


def unpack_weight(words, scales, fmt):
    g, p, n, _ = words.shape
    if fmt == "e4m3":
        vals = np.ascontiguousarray(words).view(ml_dtypes.float8_e4m3fn).astype(np.float64)
    else:
        nib = np.empty((g, p, n, 4), np.uint8)
        nib[..., 0::2] = words & 0xF
        nib[..., 1::2] = words >> 4
        vals = E2M1[nib]
    vals = vals * np.repeat(np.exp2(scales.astype(np.float64) - 127.0), 8, axis=1)[..., None]
    return vals.transpose(0, 1, 3, 2).reshape(g * 512, n)

def pack4(w):
    words, scales = pack_weight(w, "e2m1")
    return words.reshape(words.shape[0], 128, -1), scales


def unpack4(words, scales):
    return unpack_weight(words.reshape(words.shape[0], 128, -1, 2), scales, "e2m1")


B, S, HID, H, KV, D, T = 1, 512, 2048, 16, 2, 128, 512
DQ = H * D
DKV = KV * D
OUT = DQ + 2 * DKV
THETA = 1e4


def make_pos_emb():
    i = np.repeat(np.arange(D // 2), 2)
    freq = np.power(THETA, -i * 2.0 / D)
    t = freq[:, None] * f64(np.arange(T))[None, :]
    cos = np.cos(t)
    sin = np.sin(t)
    sin[0::2] *= -1.0
    return np.concatenate([cos, sin], axis=0).T


def flip_pairs(x):
    return x.reshape(x.shape[:-1] + (D // 2, 2))[..., ::-1].reshape(x.shape)


def apply_rope(x, pe):
    return x * pe[:, :D] + flip_pairs(x) * pe[:, D:]


def setup_inputs():
    s = mx_kscale(HID)
    tensor = bf(np.random.standard_normal((B, S, HID)) * s)
    w = np.random.standard_normal((OUT, HID)) * 1.5 / np.sqrt(HID) / s[None, :]
    words, scales = pack4(np.ascontiguousarray(w.T))
    return {"tensor": tensor,
            "w_qkv_words": words,
            "w_qkv_scales": scales,
            "b_qkv": bf(np.random.standard_normal(OUT) * 0.3),
            "pos_emb": bf(make_pos_emb())}


def reference(tensor, w_qkv_words, w_qkv_scales, b_qkv, pos_emb):
    qkv = (mxq(f64(tensor), 2, "e5m2") @ unpack4(w_qkv_words, w_qkv_scales)) + f64(b_qkv)
    q = qkv[..., :DQ].reshape(B, S, H, D).transpose(0, 2, 1, 3)
    k = qkv[..., DQ:DQ + DKV].reshape(B, S, KV, D).transpose(0, 2, 1, 3)
    v = qkv[..., DQ + DKV:].reshape(B, S, KV, D).transpose(0, 2, 1, 3)
    pe = f64(pos_emb)[:S]
    return apply_rope(q, pe), apply_rope(k, pe), v

@@ -1,0 +1,289 @@
+from contextlib import ExitStack
+
+import concourse.mybir as mybir
+from concourse.masks import make_identity
+
+F32 = mybir.dt.float32
+BF16 = mybir.dt.bfloat16
+I32 = mybir.dt.int32
+U32 = mybir.dt.uint32
+U8 = mybir.dt.uint8
+E5M2X4 = mybir.dt.float8_e5m2_x4
+E2M1X4 = mybir.dt.float4_e2m1fn_x4
+ADD = mybir.AluOpType.add
+MULT = mybir.AluOpType.mult
+IDENTITY = mybir.ActivationFunctionType.Identity
+
+S, HID, H, KV, D = 512, 2048, 16, 2, 128
+P = 128
+PASSES = HID // 512
+TILES = S // P
+HEADS = H + 2 * KV
+ROPE_HEADS = H + KV
+OUT = HEADS * D
+BANK = 512
+TOKEN_HEADS = 6
+SINGLE_HEADS = 2
+
+FLOPS = 2 * S * HID * OUT
+
+
+def tile_multiqueryattention_pa_kernel(tc, tensor, w_words, w_scales, b_qkv, pos_emb, out_0, out_1, out_2):
+    nc = tc.nc
+    t_cols = TOKEN_HEADS * D
+    f_heads = list(range(TOKEN_HEADS, ROPE_HEADS))
+    v_col0 = ROPE_HEADS * D
+    v_cols = KV * D
+
+    def head_out(h):
+        dst = out_0[0, h] if h < H else out_1[0, h - H]
+        return dst.rearrange("(p j) d -> p (j d)", j=TILES)
+
+    def pairs(ap):
+        return ap.rearrange("p a (n two) -> p a n two", two=2)
+
+    with ExitStack() as ctx:
+        keep = ctx.enter_context(tc.tile_pool(name="keep", bufs=1))
+        work = ctx.enter_context(tc.tile_pool(name="work", bufs=2))
+        psum = ctx.enter_context(tc.psum_pool(name="psum", bufs=1))
+        ctx.enter_context(tc.manual_schedule())
+
+        def bank(i):
+            return psum.tile([P, BANK], F32, name="bank%d" % i, tag="bank%d" % i)
+
+        b_rows = keep.tile([P, D], BF16, name="b_rows")
+        nc.gpsimd.memset(b_rows[:], 0.0)
+        ident = keep.tile([P, P], F32, name="ident")
+        make_identity(nc, ident[:])
+        nc.scalar.dma_start(out=b_rows[0:HEADS, :], in_=b_qkv.rearrange("(h d) -> h d", d=D))
+        pe = keep.tile([P, TILES, 2 * D], BF16, name="pe")
+        ident_bf = keep.tile([P, P], BF16, name="ident_bf")
+        nc.scalar.activation(out=ident_bf[:], in_=ident[:], func=IDENTITY)
+
+        x_rows = tensor[0].rearrange("(p j) k -> p j k", j=TILES)
+        x_sb = [keep.tile([P, HID], BF16, name="x%d" % j) for j in range(TILES)]
+
+        def load_x(j):
+            nc.sync.dma_start(out=x_sb[j][:], in_=x_rows[:, j, :])
+
+        def load_scales(name, c0, c1):
+            plane = keep.tile([P, PASSES, c1 - c0], U8, name=name, align_bytes=64)
+            for q in range(4):
+                nc.sync.dma_start(
+                    out=plane[32 * q : 32 * q + 4, :, :].bitcast(I32),
+                    in_=w_scales[:, 4 * q : 4 * q + 4, c0:c1].rearrange("g r n -> r g n").bitcast(I32),
+                )
+            return plane
+
+        def load_words(name, g0, g1, c0, c1):
+            words = keep.tile([P, g1 - g0, 2 * (c1 - c0)], U8, name=name, align_bytes=64)
+            nc.sync.dma_start(
+                out=words[:].bitcast(I32),
+                in_=w_words[g0:g1, :, 2 * c0 : 2 * c1].rearrange("g p n -> p g n").bitcast(I32),
+            )
+            return words
+
+        load_x(0)
+        load_x(1)
+        plane_t = load_scales("plane_t", 0, t_cols)
+        words_t = [load_words("words_t%d" % i, 2 * i, 2 * i + 2, 0, t_cols) for i in range(2)]
+        load_x(2)
+        nc.sync.dma_start(out=pe[:], in_=pos_emb.rearrange("(p j) c -> p j c", j=TILES))
+        load_x(3)
+        plane_f = load_scales("plane_f", t_cols, OUT)
+        f_edges = list(range(t_cols, v_col0, 4 * D)) + [OUT]
+        words_f = [load_words("words_f%d" % i, 0, PASSES, f_edges[i], f_edges[i + 1]) for i in range(len(f_edges) - 1)]
+
+        def weight(g, c0, c1):
+            if c0 < t_cols:
+                return words_t[g // 2][:, g % 2, 2 * c0 : 2 * c1].bitcast(E2M1X4), plane_t[:, g, c0:c1]
+            i = min((c0 - t_cols) // (4 * D), len(words_f) - 1)
+            e = f_edges[i]
+            return words_f[i][:, g, 2 * (c0 - e) : 2 * (c1 - e)].bitcast(E2M1X4), plane_f[:, g, c0 - t_cols : c1 - t_cols]
+
+        codes = [keep.tile([P, S], U32, name="codes%d" % g, align_bytes=64) for g in range(PASSES)]
+        scales = [keep.tile([P, S], U8, name="scales%d" % g, align_bytes=64) for g in range(PASSES)]
+        grouped = {}
+
+        def transpose_x(j):
+            words = x_sb[j][:].bitcast(F32)
+            grouped[j] = work.tile([P, PASSES, P * 4], BF16, name="grouped", align_bytes=64)
+            for half in range(2):
+                xt = bank(2 * (j % 2) + half)
+                xt4 = xt[:].rearrange("p (g u r) -> p g u r", g=2, u=2)
+                for gg in range(2):
+                    g = 2 * half + gg
+                    for u in range(2):
+                        nc.tensor.transpose(xt4[:, gg, u, :], words[:, 256 * g + u : 256 * (g + 1) : 2], ident[:])
+                dst = grouped[j][:, 2 * half : 2 * half + 2, :].bitcast(F32).rearrange("p g (r u) -> p g r u", u=2)
+                nc.scalar.copy(out=dst, in_=xt4.rearrange("p g u r -> p g r u"))
+
+        def quantize_x(j):
+            for g in range(PASSES):
+                nc.vector.quantize_mx(
+                    out=codes[g][:, P * j : P * (j + 1)].bitcast(E5M2X4),
+                    scales=scales[g][:, P * j : P * (j + 1)],
+                    in_=grouped[j][:, g, :],
+                )
+
+        bias_wide = keep.tile([P, t_cols + v_cols], F32, name="bias_wide")
+        bias_col = keep.tile([P, len(f_heads)], F32, name="bias_col")
+
+        def spread_bias():
+            acc = bank(5)
+            nc.tensor.matmul(
+                acc[:, : len(f_heads)], lhsT=b_rows[:], rhs=ident_bf[:, TOKEN_HEADS:ROPE_HEADS], start=True, stop=True
+            )
+            nc.vector.tensor_copy(out=bias_col[:], in_=acc[:, : len(f_heads)])
+            wide_heads = list(range(TOKEN_HEADS)) + list(range(ROPE_HEADS, HEADS))
+            for i0 in range(0, len(wide_heads), 4):
+                group = wide_heads[i0 : i0 + 4]
+                acc = bank(6 + i0 // 4)
+                for i, h in enumerate(group):
+                    nc.tensor.matmul(
+                        acc[:, D * i : D * (i + 1)],
+                        lhsT=ident_bf[:, h : h + 1].to_broadcast([P, P]),
+                        rhs=b_rows[:],
+                        start=True,
+                        stop=True,
+                    )
+                nc.vector.tensor_copy(out=bias_wide[:, D * i0 : D * (i0 + len(group))], in_=acc[:, : D * len(group)])
+
+        def project_tokens(acc, j, c0, c1):
+            for g in range(PASSES):
+                w, w_scale = weight(g, c0, c1)
+                nc.tensor.matmul_mx(
+                    out=acc[:, : c1 - c0],
+                    lhsT=codes[g][:, P * j : P * (j + 1)].bitcast(E5M2X4),
+                    lhsT_scale=scales[g][:, P * j : P * (j + 1)],
+                    rhs=w,
+                    rhs_scale=w_scale,
+                    start=(g == 0),
+                    stop=(g == PASSES - 1),
+                )
+
+        z_t, a_t, b_t = {}, {}, {}
+
+        def token_project(j):
+            z_t[j] = work.tile([P, t_cols], F32, name="z_t")
+            for i, c0 in enumerate(range(0, t_cols, BANK)):
+                c1 = min(c0 + BANK, t_cols)
+                acc = bank(4 + 2 * (j % 2) + i)
+                project_tokens(acc, j, c0, c1)
+                nc.vector.tensor_tensor(out=z_t[j][:, c0:c1], in0=acc[:, : c1 - c0], in1=bias_wide[:, c0:c1], op=ADD)
+
+        def token_products(j):
+            z = z_t[j][:].rearrange("p (h d) -> p h d", d=D)
+            a_t[j] = work.tile([P, TOKEN_HEADS, D], F32, name="a_t")
+            b_t[j] = work.tile([P, TOKEN_HEADS, D], F32, name="b_t")
+            cos = pe[:, j : j + 1, 0:D].to_broadcast([P, TOKEN_HEADS, D])
+            sin = pe[:, j : j + 1, D : 2 * D].to_broadcast([P, TOKEN_HEADS, D])
+            nc.vector.tensor_tensor(out=a_t[j][:], in0=z, in1=cos, op=MULT)
+            nc.vector.tensor_tensor(out=pairs(b_t[j][:]), in0=pairs(z)[:, :, :, ::-1], in1=pairs(sin), op=MULT)
+
+        def token_sum(j):
+            y_t = work.tile([P, TOKEN_HEADS, D], F32, name="y_t", bufs=TILES)
+            nc.vector.tensor_tensor(out=y_t[:], in0=a_t[j][:], in1=b_t[j][:], op=ADD)
+            nc.sync.dma_start(out=out_0[0, 0:TOKEN_HEADS].rearrange("h (p j) d -> p h j d", j=TILES)[:, :, j, :], in_=y_t[:])
+
+        z_f = {}
+
+        def feature_project(h):
+            i = h - TOKEN_HEADS
+            acc = bank(i % 4)
+            for g in range(PASSES):
+                w, w_scale = weight(g, D * h, D * (h + 1))
+                nc.tensor.matmul_mx(
+                    out=acc[:],
+                    lhsT=w,
+                    lhsT_scale=w_scale,
+                    rhs=codes[g][:].bitcast(E5M2X4),
+                    rhs_scale=scales[g][:],
+                    start=(g == 0),
+                    stop=(g == PASSES - 1),
+                )
+            z_f[h] = work.tile([P, S], F32, name="z_f", bufs=4)
+            nc.scalar.activation(out=z_f[h][:], in_=acc[:], func=IDENTITY, bias=bias_col[:, i : i + 1])
+
+        turned = {}
+
+        def feature_turn(h):
+            turned[h] = bank(4 + (h - TOKEN_HEADS) % 4)
+            for j in range(TILES):
+                nc.tensor.transpose(turned[h][:, D * j : D * (j + 1)], z_f[h][:, P * j : P * (j + 1)], ident[:])
+
+        a_f, b_f = {}, {}
+
+        def feature_products(h):
+            z = turned[h][:].rearrange("p (j d) -> p j d", d=D)
+            a_f[h] = work.tile([P, TILES, D], F32, name="a_f", bufs=3)
+            b_f[h] = work.tile([P, TILES, D], F32, name="b_f", bufs=3)
+            nc.vector.tensor_tensor(out=a_f[h][:], in0=z, in1=pe[:, :, 0:D], op=MULT)
+            nc.vector.tensor_tensor(
+                out=pairs(b_f[h][:]), in0=pairs(z)[:, :, :, ::-1], in1=pairs(pe[:, :, D : 2 * D]), op=MULT
+            )
+
+        def feature_sum(h, engine):
+            y_f = work.tile([P, TILES * D], F32, name="y_f", bufs=4)
+            engine.tensor_tensor(
+                out=y_f[:], in0=a_f[h][:].rearrange("p j d -> p (j d)"), in1=b_f[h][:].rearrange("p j d -> p (j d)"), op=ADD
+            )
+            nc.sync.dma_start(out=head_out(h), in_=y_f[:])
+
+        v_acc = {}
+
+        def value_project(j):
+            v_acc[j] = bank((len(f_heads) + j) % 4)
+            project_tokens(v_acc[j], j, v_col0, OUT)
+
+        def value_bias(j):
+            y_v = work.tile([P, KV, D], F32, name="y_v", bufs=TILES)
+            nc.vector.tensor_tensor(
+                out=y_v[:],
+                in0=v_acc[j][:, :v_cols].rearrange("p (h d) -> p h d", d=D),
+                in1=bias_wide[:, t_cols:].rearrange("p (h d) -> p h d", d=D),
+                op=ADD,
+            )
+            nc.sync.dma_start(out=out_2[0].rearrange("h (p j) d -> p h j d", j=TILES)[:, :, j, :], in_=y_v[:])
+
+        transpose_x(0)
+        quantize_x(0)
+        spread_bias()
+        transpose_x(1)
+        quantize_x(1)
+        for j in range(TILES):
+            token_project(j)
+            if j > 0:
+                token_sum(j - 1)
+            if j == 1:
+                transpose_x(3)
+                quantize_x(3)
+            token_products(j)
+            if j == 0:
+                transpose_x(2)
+                quantize_x(2)
+
+        paired = f_heads[: len(f_heads) - SINGLE_HEADS]
+        groups = [paired[i : i + 2] for i in range(0, len(paired), 2)] + [[h] for h in f_heads[len(paired) :]]
+        for h in groups[0]:
+            feature_project(h)
+        for i, group in enumerate(groups):
+            if i + 1 < len(groups):
+                for h in groups[i + 1]:
+                    feature_project(h)
+            else:
+                value_project(0)
+            for h in group:
+                feature_turn(h)
+            for h in group:
+                feature_products(h)
+                if h == f_heads[0]:
+                    token_sum(TILES - 1)
+                if h != f_heads[-1]:
+                    feature_sum(h, nc.gpsimd)
+        for j in range(1, TILES):
+            value_project(j)
+        value_bias(0)
+        feature_sum(f_heads[-1], nc.vector)
+        for j in range(1, TILES):
+            value_bias(j)

@@ -22,22 +22,25 @@ HEADS = H + 2 * KV
 ROPE_HEADS = H + KV
 OUT = HEADS * D
 BANK = 512
-TOKEN_HEADS = 6
-SINGLE_HEADS = 2
+CHUNK_HEADS = BANK // D
+CHUNKS = OUT // BANK
+TOKEN_CHUNKS = 2
+TOKEN_HEADS = TOKEN_CHUNKS * CHUNK_HEADS
 
 FLOPS = 2 * S * HID * OUT
 
 
 def tile_multiqueryattention_pa_kernel(tc, tensor, w_words, w_scales, b_qkv, pos_emb, out_0, out_1, out_2):
     nc = tc.nc
-    t_cols = TOKEN_HEADS * D
-    f_heads = list(range(TOKEN_HEADS, ROPE_HEADS))
-    v_col0 = ROPE_HEADS * D
-    v_cols = KV * D
 
     def head_out(h):
-        dst = out_0[0, h] if h < H else out_1[0, h - H]
-        return dst.rearrange("(p j) d -> p (j d)", j=TILES)
+        if h < H:
+            dst = out_0[0, h]
+        elif h < ROPE_HEADS:
+            dst = out_1[0, h - H]
+        else:
+            dst = out_2[0, h - ROPE_HEADS]
+        return dst.rearrange("(p j) d -> p j d", j=TILES)
 
     def pairs(ap):
         return ap.rearrange("p a (n two) -> p a n two", two=2)
@@ -51,20 +54,32 @@ def tile_multiqueryattention_pa_kernel(tc, tensor, w_words, w_scales, b_qkv, pos
         def bank(i):
             return psum.tile([P, BANK], F32, name="bank%d" % i, tag="bank%d" % i)
 
+        sums_opened = []
+
+        def sum_bank():
+            sums_opened.append(len(sums_opened))
+            return bank(2 + sums_opened[-1] % 4)
+
         b_rows = keep.tile([P, D], BF16, name="b_rows")
         nc.gpsimd.memset(b_rows[:], 0.0)
         ident = keep.tile([P, P], F32, name="ident")
         make_identity(nc, ident[:])
         nc.scalar.dma_start(out=b_rows[0:HEADS, :], in_=b_qkv.rearrange("(h d) -> h d", d=D))
-        pe = keep.tile([P, TILES, 2 * D], BF16, name="pe")
         ident_bf = keep.tile([P, P], BF16, name="ident_bf")
         nc.scalar.activation(out=ident_bf[:], in_=ident[:], func=IDENTITY)
 
         x_rows = tensor[0].rearrange("(p j) k -> p j k", j=TILES)
-        x_sb = [keep.tile([P, HID], BF16, name="x%d" % j) for j in range(TILES)]
+        x_halves = {}
+        table = keep.tile([P, TILES, 2 * D], BF16, name="table")
 
-        def load_x(j):
-            nc.sync.dma_start(out=x_sb[j][:], in_=x_rows[:, j, :])
+        def load_x(j, pieces):
+            width = HID // pieces
+            tiles = [keep.tile([P, width], BF16, name="x%d_%d" % (j, i)) for i in range(pieces)]
+            for i in range(pieces):
+                nc.sync.dma_start(out=tiles[i][:], in_=x_rows[:, j, width * i : width * (i + 1)])
+            for half in range(2):
+                start = half * HID // 2
+                x_halves[j, half] = tiles[start // width][:, start % width : start % width + HID // 2]
 
         def load_scales(name, c0, c1):
             plane = keep.tile([P, PASSES, c1 - c0], U8, name=name, align_bytes=64)
@@ -75,48 +90,44 @@ def tile_multiqueryattention_pa_kernel(tc, tensor, w_words, w_scales, b_qkv, pos
                 )
             return plane
 
-        def load_words(name, g0, g1, c0, c1):
-            words = keep.tile([P, g1 - g0, 2 * (c1 - c0)], U8, name=name, align_bytes=64)
+        def load_words(g0, g1, c):
+            words = keep.tile([P, g1 - g0, 2 * BANK], U8, name="words%d_%d" % (c, g0), align_bytes=64)
             nc.sync.dma_start(
                 out=words[:].bitcast(I32),
-                in_=w_words[g0:g1, :, 2 * c0 : 2 * c1].rearrange("g p n -> p g n").bitcast(I32),
+                in_=w_words[g0:g1, :, 2 * BANK * c : 2 * BANK * (c + 1)].rearrange("g p n -> p g n").bitcast(I32),
             )
-            return words
+            return [words[:, g, :] for g in range(g1 - g0)]
 
-        load_x(0)
-        load_x(1)
-        plane_t = load_scales("plane_t", 0, t_cols)
-        words_t = [load_words("words_t%d" % i, 2 * i, 2 * i + 2, 0, t_cols) for i in range(2)]
-        load_x(2)
-        nc.sync.dma_start(out=pe[:], in_=pos_emb.rearrange("(p j) c -> p j c", j=TILES))
-        load_x(3)
-        plane_f = load_scales("plane_f", t_cols, OUT)
-        f_edges = list(range(t_cols, v_col0, 4 * D)) + [OUT]
-        words_f = [load_words("words_f%d" % i, 0, PASSES, f_edges[i], f_edges[i + 1]) for i in range(len(f_edges) - 1)]
+        load_x(0, 2)
+        load_x(1, 1)
+        plane_first = load_scales("plane_first", 0, BANK)
+        words = {0: load_words(0, 2, 0) + load_words(2, 4, 0)}
+        nc.sync.dma_start(out=table[:], in_=pos_emb.rearrange("(p j) c -> p j c", j=TILES))
+        load_x(2, 1)
+        load_x(3, 1)
+        plane_rest = load_scales("plane_rest", BANK, OUT)
+        for c in (2, 1, 3, 4):
+            words[c] = load_words(0, PASSES, c)
 
         def weight(g, c0, c1):
-            if c0 < t_cols:
-                return words_t[g // 2][:, g % 2, 2 * c0 : 2 * c1].bitcast(E2M1X4), plane_t[:, g, c0:c1]
-            i = min((c0 - t_cols) // (4 * D), len(words_f) - 1)
-            e = f_edges[i]
-            return words_f[i][:, g, 2 * (c0 - e) : 2 * (c1 - e)].bitcast(E2M1X4), plane_f[:, g, c0 - t_cols : c1 - t_cols]
+            c = c0 // BANK
+            scale = plane_first[:, g, c0:c1] if c == 0 else plane_rest[:, g, c0 - BANK : c1 - BANK]
+            return words[c][g][:, 2 * (c0 - BANK * c) : 2 * (c1 - BANK * c)].bitcast(E2M1X4), scale
 
         codes = [keep.tile([P, S], U32, name="codes%d" % g, align_bytes=64) for g in range(PASSES)]
         scales = [keep.tile([P, S], U8, name="scales%d" % g, align_bytes=64) for g in range(PASSES)]
         grouped = {}
 
         def transpose_x(j):
-            words = x_sb[j][:].bitcast(F32)
             grouped[j] = work.tile([P, PASSES, P * 4], BF16, name="grouped", align_bytes=64)
             for half in range(2):
-                xt = bank(2 * (j % 2) + half)
-                xt4 = xt[:].rearrange("p (g u r) -> p g u r", g=2, u=2)
+                x_words = x_halves[j, half].bitcast(F32)
+                xt = bank(half)[:].rearrange("p (g u r) -> p g u r", g=2, u=2)
                 for gg in range(2):
-                    g = 2 * half + gg
                     for u in range(2):
-                        nc.tensor.transpose(xt4[:, gg, u, :], words[:, 256 * g + u : 256 * (g + 1) : 2], ident[:])
+                        nc.tensor.transpose(xt[:, gg, u, :], x_words[:, 256 * gg + u : 256 * (gg + 1) : 2], ident[:])
                 dst = grouped[j][:, 2 * half : 2 * half + 2, :].bitcast(F32).rearrange("p g (r u) -> p g r u", u=2)
-                nc.scalar.copy(out=dst, in_=xt4.rearrange("p g u r -> p g r u"))
+                nc.scalar.copy(out=dst, in_=xt.rearrange("p g u r -> p g r u"))
 
         def quantize_x(j):
             for g in range(PASSES):
@@ -126,20 +137,14 @@ def tile_multiqueryattention_pa_kernel(tc, tensor, w_words, w_scales, b_qkv, pos
                     in_=grouped[j][:, g, :],
                 )
 
-        bias_wide = keep.tile([P, t_cols + v_cols], F32, name="bias_wide")
-        bias_col = keep.tile([P, len(f_heads)], F32, name="bias_col")
+        bias_wide = keep.tile([P, TOKEN_CHUNKS, BANK], F32, name="bias_wide")
+        bias_col = keep.tile([P, HEADS - TOKEN_HEADS], F32, name="bias_col")
 
         def spread_bias():
-            acc = bank(5)
-            nc.tensor.matmul(
-                acc[:, : len(f_heads)], lhsT=b_rows[:], rhs=ident_bf[:, TOKEN_HEADS:ROPE_HEADS], start=True, stop=True
-            )
-            nc.vector.tensor_copy(out=bias_col[:], in_=acc[:, : len(f_heads)])
-            wide_heads = list(range(TOKEN_HEADS)) + list(range(ROPE_HEADS, HEADS))
-            for i0 in range(0, len(wide_heads), 4):
-                group = wide_heads[i0 : i0 + 4]
-                acc = bank(6 + i0 // 4)
-                for i, h in enumerate(group):
+            for c in range(TOKEN_CHUNKS):
+                acc = bank(3 + c)
+                for i in range(CHUNK_HEADS):
+                    h = CHUNK_HEADS * c + i
                     nc.tensor.matmul(
                         acc[:, D * i : D * (i + 1)],
                         lhsT=ident_bf[:, h : h + 1].to_broadcast([P, P]),
@@ -147,13 +152,43 @@ def tile_multiqueryattention_pa_kernel(tc, tensor, w_words, w_scales, b_qkv, pos
                         start=True,
                         stop=True,
                     )
-                nc.vector.tensor_copy(out=bias_wide[:, D * i0 : D * (i0 + len(group))], in_=acc[:, : D * len(group)])
+                nc.vector.tensor_copy(out=bias_wide[:, c, :], in_=acc[:])
+            acc = bank(6)
+            n = HEADS - TOKEN_HEADS
+            nc.tensor.matmul(acc[:, :n], lhsT=b_rows[:], rhs=ident_bf[:, TOKEN_HEADS:HEADS], start=True, stop=True)
+            nc.vector.tensor_copy(out=bias_col[:], in_=acc[:, :n])
 
-        def project_tokens(acc, j, c0, c1):
+        table_ps = psum.tile([P, TILES, 2 * D], BF16, name="table_ps")
+
+        def table_to_psum():
+            for half in range(2):
+                js = slice(2 * half, 2 * half + 2)
+                nc.tensor.matmul(
+                    table_ps[:, js, :].rearrange("p j c -> p (j c)"),
+                    lhsT=ident_bf[:],
+                    rhs=table[:, js, :].rearrange("p j c -> p (j c)"),
+                    start=True,
+                    stop=True,
+                )
+
+        def rope_products(z, cos, sin):
+            a = work.tile([P, 4, D], F32, name="a", bufs=4)
+            b = work.tile([P, 4, D], F32, name="b", bufs=4)
+            nc.vector.tensor_tensor(out=a[:], in0=z, in1=cos, op=MULT)
+            nc.vector.tensor_tensor(out=pairs(b[:]), in0=pairs(z)[:, :, :, ::-1], in1=pairs(sin), op=MULT)
+            return a, b
+
+        def rope_sum(engine, products, dst):
+            y = work.tile([P, 4, D], F32, name="y", bufs=5)
+            engine.tensor_tensor(out=y[:], in0=products[0][:], in1=products[1][:], op=ADD)
+            nc.sync.dma_start(out=dst, in_=y[:])
+
+        def token_project(c, j):
+            acc = sum_bank()
             for g in range(PASSES):
-                w, w_scale = weight(g, c0, c1)
+                w, w_scale = weight(g, BANK * c, BANK * (c + 1))
                 nc.tensor.matmul_mx(
-                    out=acc[:, : c1 - c0],
+                    out=acc[:],
                     lhsT=codes[g][:, P * j : P * (j + 1)].bitcast(E5M2X4),
                     lhsT_scale=scales[g][:, P * j : P * (j + 1)],
                     rhs=w,
@@ -161,36 +196,21 @@ def tile_multiqueryattention_pa_kernel(tc, tensor, w_words, w_scales, b_qkv, pos
                     start=(g == 0),
                     stop=(g == PASSES - 1),
                 )
+            z = work.tile([P, CHUNK_HEADS, D], F32, name="z_token", bufs=3)
+            nc.vector.tensor_tensor(out=z[:].rearrange("p h d -> p (h d)"), in0=acc[:], in1=bias_wide[:, c, :], op=ADD)
+            return z
 
-        z_t, a_t, b_t = {}, {}, {}
+        def token_products(z, j, source):
+            cos = source[:, j : j + 1, 0:D].to_broadcast([P, CHUNK_HEADS, D])
+            sin = source[:, j : j + 1, D : 2 * D].to_broadcast([P, CHUNK_HEADS, D])
+            return rope_products(z[:], cos, sin)
 
-        def token_project(j):
-            z_t[j] = work.tile([P, t_cols], F32, name="z_t")
-            for i, c0 in enumerate(range(0, t_cols, BANK)):
-                c1 = min(c0 + BANK, t_cols)
-                acc = bank(4 + 2 * (j % 2) + i)
-                project_tokens(acc, j, c0, c1)
-                nc.vector.tensor_tensor(out=z_t[j][:, c0:c1], in0=acc[:, : c1 - c0], in1=bias_wide[:, c0:c1], op=ADD)
-
-        def token_products(j):
-            z = z_t[j][:].rearrange("p (h d) -> p h d", d=D)
-            a_t[j] = work.tile([P, TOKEN_HEADS, D], F32, name="a_t")
-            b_t[j] = work.tile([P, TOKEN_HEADS, D], F32, name="b_t")
-            cos = pe[:, j : j + 1, 0:D].to_broadcast([P, TOKEN_HEADS, D])
-            sin = pe[:, j : j + 1, D : 2 * D].to_broadcast([P, TOKEN_HEADS, D])
-            nc.vector.tensor_tensor(out=a_t[j][:], in0=z, in1=cos, op=MULT)
-            nc.vector.tensor_tensor(out=pairs(b_t[j][:]), in0=pairs(z)[:, :, :, ::-1], in1=pairs(sin), op=MULT)
-
-        def token_sum(j):
-            y_t = work.tile([P, TOKEN_HEADS, D], F32, name="y_t", bufs=TILES)
-            nc.vector.tensor_tensor(out=y_t[:], in0=a_t[j][:], in1=b_t[j][:], op=ADD)
-            nc.sync.dma_start(out=out_0[0, 0:TOKEN_HEADS].rearrange("h (p j) d -> p h j d", j=TILES)[:, :, j, :], in_=y_t[:])
-
-        z_f = {}
+        def token_out(c, j):
+            heads = out_0[0, CHUNK_HEADS * c : CHUNK_HEADS * (c + 1)]
+            return heads.rearrange("h (p j) d -> p h j d", j=TILES)[:, :, j, :]
 
         def feature_project(h):
-            i = h - TOKEN_HEADS
-            acc = bank(i % 4)
+            acc = sum_bank()
             for g in range(PASSES):
                 w, w_scale = weight(g, D * h, D * (h + 1))
                 nc.tensor.matmul_mx(
@@ -202,88 +222,64 @@ def tile_multiqueryattention_pa_kernel(tc, tensor, w_words, w_scales, b_qkv, pos
                     start=(g == 0),
                     stop=(g == PASSES - 1),
                 )
-            z_f[h] = work.tile([P, S], F32, name="z_f", bufs=4)
-            nc.scalar.activation(out=z_f[h][:], in_=acc[:], func=IDENTITY, bias=bias_col[:, i : i + 1])
+            z = work.tile([P, S], F32, name="z_feature", bufs=4)
+            i = h - TOKEN_HEADS
+            nc.scalar.activation(out=z[:], in_=acc[:], func=IDENTITY, bias=bias_col[:, i : i + 1])
+            return z
 
-        turned = {}
-
-        def feature_turn(h):
-            turned[h] = bank(4 + (h - TOKEN_HEADS) % 4)
+        def feature_turn(h, z):
+            turned = bank((6, 0, 1)[(h - TOKEN_HEADS) % 3])[:].rearrange("p (j d) -> p j d", d=D)
             for j in range(TILES):
-                nc.tensor.transpose(turned[h][:, D * j : D * (j + 1)], z_f[h][:, P * j : P * (j + 1)], ident[:])
+                nc.tensor.transpose(turned[:, j, :], z[:, P * j : P * (j + 1)], ident[:])
+            return turned
 
-        a_f, b_f = {}, {}
+        def feature_products(turned):
+            return rope_products(turned, table[:, :, 0:D], table[:, :, D : 2 * D])
 
-        def feature_products(h):
-            z = turned[h][:].rearrange("p (j d) -> p j d", d=D)
-            a_f[h] = work.tile([P, TILES, D], F32, name="a_f", bufs=3)
-            b_f[h] = work.tile([P, TILES, D], F32, name="b_f", bufs=3)
-            nc.vector.tensor_tensor(out=a_f[h][:], in0=z, in1=pe[:, :, 0:D], op=MULT)
-            nc.vector.tensor_tensor(
-                out=pairs(b_f[h][:]), in0=pairs(z)[:, :, :, ::-1], in1=pairs(pe[:, :, D : 2 * D]), op=MULT
-            )
-
-        def feature_sum(h, engine):
-            y_f = work.tile([P, TILES * D], F32, name="y_f", bufs=4)
-            engine.tensor_tensor(
-                out=y_f[:], in0=a_f[h][:].rearrange("p j d -> p (j d)"), in1=b_f[h][:].rearrange("p j d -> p (j d)"), op=ADD
-            )
-            nc.sync.dma_start(out=head_out(h), in_=y_f[:])
-
-        v_acc = {}
-
-        def value_project(j):
-            v_acc[j] = bank((len(f_heads) + j) % 4)
-            project_tokens(v_acc[j], j, v_col0, OUT)
-
-        def value_bias(j):
-            y_v = work.tile([P, KV, D], F32, name="y_v", bufs=TILES)
-            nc.vector.tensor_tensor(
-                out=y_v[:],
-                in0=v_acc[j][:, :v_cols].rearrange("p (h d) -> p h d", d=D),
-                in1=bias_wide[:, t_cols:].rearrange("p (h d) -> p h d", d=D),
-                op=ADD,
-            )
-            nc.sync.dma_start(out=out_2[0].rearrange("h (p j) d -> p h j d", j=TILES)[:, :, j, :], in_=y_v[:])
+        def value_store(h, turned):
+            y = work.tile([P, TILES, D], F32, name="y_value")
+            nc.scalar.copy(out=y[:], in_=turned)
+            nc.sync.dma_start(out=head_out(h), in_=y[:])
 
         transpose_x(0)
         quantize_x(0)
         spread_bias()
         transpose_x(1)
         quantize_x(1)
-        for j in range(TILES):
-            token_project(j)
-            if j > 0:
-                token_sum(j - 1)
-            if j == 1:
-                transpose_x(3)
-                quantize_x(3)
-            token_products(j)
-            if j == 0:
-                transpose_x(2)
-                quantize_x(2)
+        z0 = token_project(0, 0)
+        transpose_x(2)
+        products = token_products(z0, 0, table)
+        quantize_x(2)
+        rope_sum(nc.vector, products, token_out(0, 0))
+        z1 = token_project(0, 1)
+        transpose_x(3)
+        products = token_products(z1, 1, table)
+        quantize_x(3)
+        rope_sum(nc.vector, products, token_out(0, 1))
+        z2 = token_project(0, 2)
+        table_to_psum()
+        products = token_products(z2, 2, table_ps)
+        z3 = token_project(0, 3)
+        rope_sum(nc.gpsimd, products, token_out(0, 2))
+        rope_sum(nc.gpsimd, token_products(z3, 3, table_ps), token_out(0, 3))
 
-        paired = f_heads[: len(f_heads) - SINGLE_HEADS]
-        groups = [paired[i : i + 2] for i in range(0, len(paired), 2)] + [[h] for h in f_heads[len(paired) :]]
-        for h in groups[0]:
-            feature_project(h)
-        for i, group in enumerate(groups):
-            if i + 1 < len(groups):
-                for h in groups[i + 1]:
-                    feature_project(h)
-            else:
-                value_project(0)
-            for h in group:
-                feature_turn(h)
-            for h in group:
-                feature_products(h)
-                if h == f_heads[0]:
-                    token_sum(TILES - 1)
-                if h != f_heads[-1]:
-                    feature_sum(h, nc.gpsimd)
-        for j in range(1, TILES):
-            value_project(j)
-        value_bias(0)
-        feature_sum(f_heads[-1], nc.vector)
-        for j in range(1, TILES):
-            value_bias(j)
+        for j in range(TILES):
+            first, second = TOKEN_HEADS + 2 * j, TOKEN_HEADS + 2 * j + 1
+            z_first = feature_project(first)
+            z_second = feature_project(second)
+            z = token_project(1, j)
+            turned_first = feature_turn(first, z_first)
+            turned_second = feature_turn(second, z_second)
+            rope_sum(nc.gpsimd, feature_products(turned_first), head_out(first))
+            rope_sum(nc.gpsimd, token_products(z, j, table_ps), token_out(1, j))
+            rope_sum(nc.gpsimd, feature_products(turned_second), head_out(second))
+
+        k0, k1, v0, v1 = range(H, HEADS)
+        z_k0 = feature_project(k0)
+        z_k1 = feature_project(k1)
+        rope_sum(nc.gpsimd, feature_products(feature_turn(k0, z_k0)), head_out(k0))
+        z_v0 = feature_project(v0)
+        rope_sum(nc.vector, feature_products(feature_turn(k1, z_k1)), head_out(k1))
+        z_v1 = feature_project(v1)
+        value_store(v0, feature_turn(v0, z_v0))
+        value_store(v1, feature_turn(v1, z_v1))

@@ -81,12 +81,13 @@ def tile_multiqueryattention_pa_kernel(tc, tensor, w_words, w_scales, b_qkv, pos
                 start = half * HID // 2
                 x_halves[j, half] = tiles[start // width][:, start % width : start % width + HID // 2]
 
-        def load_scales(name, c0, c1):
-            plane = keep.tile([P, PASSES, c1 - c0], U8, name=name, align_bytes=64)
-            for q in range(4):
+        def load_scales(first, count):
+            c0, c1 = BANK * first, BANK * (first + count)
+            plane = keep.tile([P, PASSES, c1 - c0], U8, name="plane%d" % first, align_bytes=64)
+            for r in range(4):
                 nc.sync.dma_start(
-                    out=plane[32 * q : 32 * q + 4, :, :].bitcast(I32),
-                    in_=w_scales[:, 4 * q : 4 * q + 4, c0:c1].rearrange("g r n -> r g n").bitcast(I32),
+                    out=plane[r:P:32, :, :].bitcast(I32),
+                    in_=w_scales[:, r:16:4, c0:c1].rearrange("g q n -> q g n").bitcast(I32),
                 )
             return plane
 
@@ -99,20 +100,22 @@ def tile_multiqueryattention_pa_kernel(tc, tensor, w_words, w_scales, b_qkv, pos
             return [words[:, g, :] for g in range(g1 - g0)]
 
         load_x(0, 2)
-        load_x(1, 1)
-        plane_first = load_scales("plane_first", 0, BANK)
-        words = {0: load_words(0, 2, 0) + load_words(2, 4, 0)}
         nc.sync.dma_start(out=table[:], in_=pos_emb.rearrange("(p j) c -> p j c", j=TILES))
+        load_x(1, 1)
+        planes = {0: load_scales(0, 1)[:]}
+        words = {0: load_words(0, 2, 0) + load_words(2, 4, 0)}
         load_x(2, 1)
         load_x(3, 1)
-        plane_rest = load_scales("plane_rest", BANK, OUT)
-        for c in (2, 1, 3, 4):
-            words[c] = load_words(0, PASSES, c)
+        for first, order in ((1, (2, 1)), (3, (3, 4))):
+            plane = load_scales(first, 2)
+            for c in order:
+                planes[c] = plane[:, :, BANK * (c - first) : BANK * (c - first + 1)]
+                words[c] = load_words(0, PASSES, c)
 
         def weight(g, c0, c1):
             c = c0 // BANK
-            scale = plane_first[:, g, c0:c1] if c == 0 else plane_rest[:, g, c0 - BANK : c1 - BANK]
-            return words[c][g][:, 2 * (c0 - BANK * c) : 2 * (c1 - BANK * c)].bitcast(E2M1X4), scale
+            lo, hi = c0 - BANK * c, c1 - BANK * c
+            return words[c][g][:, 2 * lo : 2 * hi].bitcast(E2M1X4), planes[c][:, g, lo:hi]
 
         codes = [keep.tile([P, S], U32, name="codes%d" % g, align_bytes=64) for g in range(PASSES)]
         scales = [keep.tile([P, S], U8, name="scales%d" % g, align_bytes=64) for g in range(PASSES)]
@@ -171,12 +174,15 @@ def tile_multiqueryattention_pa_kernel(tc, tensor, w_words, w_scales, b_qkv, pos
                     stop=True,
                 )
 
-        def rope_products(z, cos, sin):
+        def cos_product(z, cos):
             a = work.tile([P, 4, D], F32, name="a", bufs=4)
-            b = work.tile([P, 4, D], F32, name="b", bufs=4)
             nc.vector.tensor_tensor(out=a[:], in0=z, in1=cos, op=MULT)
+            return a
+
+        def sin_product(z, sin):
+            b = work.tile([P, 4, D], F32, name="b", bufs=4)
             nc.vector.tensor_tensor(out=pairs(b[:]), in0=pairs(z)[:, :, :, ::-1], in1=pairs(sin), op=MULT)
-            return a, b
+            return b
 
         def rope_sum(engine, products, dst):
             y = work.tile([P, 4, D], F32, name="y", bufs=5)
@@ -200,10 +206,14 @@ def tile_multiqueryattention_pa_kernel(tc, tensor, w_words, w_scales, b_qkv, pos
             nc.vector.tensor_tensor(out=z[:].rearrange("p h d -> p (h d)"), in0=acc[:], in1=bias_wide[:, c, :], op=ADD)
             return z
 
-        def token_products(z, j, source):
-            cos = source[:, j : j + 1, 0:D].to_broadcast([P, CHUNK_HEADS, D])
-            sin = source[:, j : j + 1, D : 2 * D].to_broadcast([P, CHUNK_HEADS, D])
-            return rope_products(z[:], cos, sin)
+        def token_cos(z, j):
+            return cos_product(z[:], table_ps[:, j : j + 1, 0:D].to_broadcast([P, CHUNK_HEADS, D]))
+
+        def token_sin(z, j):
+            return sin_product(z[:], table_ps[:, j : j + 1, D : 2 * D].to_broadcast([P, CHUNK_HEADS, D]))
+
+        def token_products(z, j):
+            return token_cos(z, j), token_sin(z, j)
 
         def token_out(c, j):
             heads = out_0[0, CHUNK_HEADS * c : CHUNK_HEADS * (c + 1)]
@@ -234,7 +244,7 @@ def tile_multiqueryattention_pa_kernel(tc, tensor, w_words, w_scales, b_qkv, pos
             return turned
 
         def feature_products(turned):
-            return rope_products(turned, table[:, :, 0:D], table[:, :, D : 2 * D])
+            return cos_product(turned, table[:, :, 0:D]), sin_product(turned, table[:, :, D : 2 * D])
 
         def value_store(h, turned):
             y = work.tile([P, TILES, D], F32, name="y_value")
@@ -244,24 +254,19 @@ def tile_multiqueryattention_pa_kernel(tc, tensor, w_words, w_scales, b_qkv, pos
         transpose_x(0)
         quantize_x(0)
         spread_bias()
+        table_to_psum()
         transpose_x(1)
         quantize_x(1)
-        z0 = token_project(0, 0)
-        transpose_x(2)
-        products = token_products(z0, 0, table)
-        quantize_x(2)
-        rope_sum(nc.vector, products, token_out(0, 0))
-        z1 = token_project(0, 1)
-        transpose_x(3)
-        products = token_products(z1, 1, table)
-        quantize_x(3)
-        rope_sum(nc.vector, products, token_out(0, 1))
+        for j in range(2):
+            z = token_project(0, j)
+            transpose_x(j + 2)
+            a = token_cos(z, j)
+            quantize_x(j + 2)
+            rope_sum(nc.gpsimd, (a, token_sin(z, j)), token_out(0, j))
         z2 = token_project(0, 2)
-        table_to_psum()
-        products = token_products(z2, 2, table_ps)
         z3 = token_project(0, 3)
-        rope_sum(nc.gpsimd, products, token_out(0, 2))
-        rope_sum(nc.gpsimd, token_products(z3, 3, table_ps), token_out(0, 3))
+        rope_sum(nc.gpsimd, token_products(z2, 2), token_out(0, 2))
+        rope_sum(nc.gpsimd, token_products(z3, 3), token_out(0, 3))
 
         for j in range(TILES):
             first, second = TOKEN_HEADS + 2 * j, TOKEN_HEADS + 2 * j + 1
@@ -271,7 +276,7 @@ def tile_multiqueryattention_pa_kernel(tc, tensor, w_words, w_scales, b_qkv, pos
             turned_first = feature_turn(first, z_first)
             turned_second = feature_turn(second, z_second)
             rope_sum(nc.gpsimd, feature_products(turned_first), head_out(first))
-            rope_sum(nc.gpsimd, token_products(z, j, table_ps), token_out(1, j))
+            rope_sum(nc.gpsimd, token_products(z, j), token_out(1, j))
             rope_sum(nc.gpsimd, feature_products(turned_second), head_out(second))
 
         k0, k1, v0, v1 = range(H, HEADS)

from contextlib import ExitStack

import concourse.mybir as mybir
from concourse.masks import make_identity

F32 = mybir.dt.float32
BF16 = mybir.dt.bfloat16
I32 = mybir.dt.int32
U32 = mybir.dt.uint32
U8 = mybir.dt.uint8
E5M2X4 = mybir.dt.float8_e5m2_x4
E2M1X4 = mybir.dt.float4_e2m1fn_x4
ADD = mybir.AluOpType.add
MULT = mybir.AluOpType.mult
IDENTITY = mybir.ActivationFunctionType.Identity

S, HID, H, KV, D = 512, 2048, 16, 2, 128
P = 128
PASSES = HID // 512
TILES = S // P
HEADS = H + 2 * KV
ROPE_HEADS = H + KV
OUT = HEADS * D
BANK = 512
CHUNK_HEADS = BANK // D
CHUNKS = OUT // BANK
TOKEN_CHUNKS = 2
TOKEN_HEADS = TOKEN_CHUNKS * CHUNK_HEADS

FLOPS = 2 * S * HID * OUT


def tile_multiqueryattention_pa_kernel(tc, tensor, w_words, w_scales, b_qkv, pos_emb, out_0, out_1, out_2):
    nc = tc.nc

    def head_out(h):
        if h < H:
            dst = out_0[0, h]
        elif h < ROPE_HEADS:
            dst = out_1[0, h - H]
        else:
            dst = out_2[0, h - ROPE_HEADS]
        return dst.rearrange("(p j) d -> p j d", j=TILES)

    def pairs(ap):
        return ap.rearrange("p a (n two) -> p a n two", two=2)

    with ExitStack() as ctx:
        keep = ctx.enter_context(tc.tile_pool(name="keep", bufs=1))
        work = ctx.enter_context(tc.tile_pool(name="work", bufs=2))
        psum = ctx.enter_context(tc.psum_pool(name="psum", bufs=1))
        ctx.enter_context(tc.manual_schedule())

        def bank(i):
            return psum.tile([P, BANK], F32, name="bank%d" % i, tag="bank%d" % i)

        sums_opened = []

        def sum_bank():
            sums_opened.append(len(sums_opened))
            return bank(2 + sums_opened[-1] % 4)

        b_rows = keep.tile([P, D], BF16, name="b_rows")
        nc.gpsimd.memset(b_rows[:], 0.0)
        ident = keep.tile([P, P], F32, name="ident")
        make_identity(nc, ident[:])
        nc.scalar.dma_start(out=b_rows[0:HEADS, :], in_=b_qkv.rearrange("(h d) -> h d", d=D))
        ident_bf = keep.tile([P, P], BF16, name="ident_bf")
        nc.scalar.activation(out=ident_bf[:], in_=ident[:], func=IDENTITY)

        x_rows = tensor[0].rearrange("(p j) k -> p j k", j=TILES)
        x_halves = {}
        table = keep.tile([P, TILES, 2 * D], BF16, name="table")

        def load_x(j, pieces):
            width = HID // pieces
            tiles = [keep.tile([P, width], BF16, name="x%d_%d" % (j, i)) for i in range(pieces)]
            for i in range(pieces):
                nc.sync.dma_start(out=tiles[i][:], in_=x_rows[:, j, width * i : width * (i + 1)])
            for half in range(2):
                start = half * HID // 2
                x_halves[j, half] = tiles[start // width][:, start % width : start % width + HID // 2]

        def load_scales(first, count):
            c0, c1 = BANK * first, BANK * (first + count)
            plane = keep.tile([P, PASSES, c1 - c0], U8, name="plane%d" % first, align_bytes=64)
            for r in range(4):
                nc.sync.dma_start(
                    out=plane[r:P:32, :, :].bitcast(I32),
                    in_=w_scales[:, r:16:4, c0:c1].rearrange("g q n -> q g n").bitcast(I32),
                )
            return plane

        def load_words(g0, g1, c):
            words = keep.tile([P, g1 - g0, 2 * BANK], U8, name="words%d_%d" % (c, g0), align_bytes=64)
            nc.sync.dma_start(
                out=words[:].bitcast(I32),
                in_=w_words[g0:g1, :, 2 * BANK * c : 2 * BANK * (c + 1)].rearrange("g p n -> p g n").bitcast(I32),
            )
            return [words[:, g, :] for g in range(g1 - g0)]

        load_x(0, 2)
        nc.sync.dma_start(out=table[:], in_=pos_emb.rearrange("(p j) c -> p j c", j=TILES))
        load_x(1, 1)
        planes = {0: load_scales(0, 1)[:]}
        words = {0: load_words(0, 2, 0) + load_words(2, 4, 0)}
        load_x(2, 1)
        load_x(3, 1)
        for first, order in ((1, (2, 1)), (3, (3, 4))):
            plane = load_scales(first, 2)
            for c in order:
                planes[c] = plane[:, :, BANK * (c - first) : BANK * (c - first + 1)]
                words[c] = load_words(0, PASSES, c)

        def weight(g, c0, c1):
            c = c0 // BANK
            lo, hi = c0 - BANK * c, c1 - BANK * c
            return words[c][g][:, 2 * lo : 2 * hi].bitcast(E2M1X4), planes[c][:, g, lo:hi]

        codes = [keep.tile([P, S], U32, name="codes%d" % g, align_bytes=64) for g in range(PASSES)]
        scales = [keep.tile([P, S], U8, name="scales%d" % g, align_bytes=64) for g in range(PASSES)]
        grouped = {}

        def transpose_x(j):
            grouped[j] = work.tile([P, PASSES, P * 4], BF16, name="grouped", align_bytes=64)
            for half in range(2):
                x_words = x_halves[j, half].bitcast(F32)
                xt = bank(half)[:].rearrange("p (g u r) -> p g u r", g=2, u=2)
                for gg in range(2):
                    for u in range(2):
                        nc.tensor.transpose(xt[:, gg, u, :], x_words[:, 256 * gg + u : 256 * (gg + 1) : 2], ident[:])
                dst = grouped[j][:, 2 * half : 2 * half + 2, :].bitcast(F32).rearrange("p g (r u) -> p g r u", u=2)
                nc.scalar.copy(out=dst, in_=xt.rearrange("p g u r -> p g r u"))

        def quantize_x(j):
            for g in range(PASSES):
                nc.vector.quantize_mx(
                    out=codes[g][:, P * j : P * (j + 1)].bitcast(E5M2X4),
                    scales=scales[g][:, P * j : P * (j + 1)],
                    in_=grouped[j][:, g, :],
                )

        bias_wide = keep.tile([P, TOKEN_CHUNKS, BANK], F32, name="bias_wide")
        bias_col = keep.tile([P, HEADS - TOKEN_HEADS], F32, name="bias_col")

        def spread_bias():
            for c in range(TOKEN_CHUNKS):
                acc = bank(3 + c)
                for i in range(CHUNK_HEADS):
                    h = CHUNK_HEADS * c + i
                    nc.tensor.matmul(
                        acc[:, D * i : D * (i + 1)],
                        lhsT=ident_bf[:, h : h + 1].to_broadcast([P, P]),
                        rhs=b_rows[:],
                        start=True,
                        stop=True,
                    )
                nc.vector.tensor_copy(out=bias_wide[:, c, :], in_=acc[:])
            acc = bank(6)
            n = HEADS - TOKEN_HEADS
            nc.tensor.matmul(acc[:, :n], lhsT=b_rows[:], rhs=ident_bf[:, TOKEN_HEADS:HEADS], start=True, stop=True)
            nc.vector.tensor_copy(out=bias_col[:], in_=acc[:, :n])

        table_ps = psum.tile([P, TILES, 2 * D], BF16, name="table_ps")

        def table_to_psum():
            for half in range(2):
                js = slice(2 * half, 2 * half + 2)
                nc.tensor.matmul(
                    table_ps[:, js, :].rearrange("p j c -> p (j c)"),
                    lhsT=ident_bf[:],
                    rhs=table[:, js, :].rearrange("p j c -> p (j c)"),
                    start=True,
                    stop=True,
                )

        def cos_product(z, cos):
            a = work.tile([P, 4, D], F32, name="a", bufs=4)
            nc.vector.tensor_tensor(out=a[:], in0=z, in1=cos, op=MULT)
            return a

        def sin_product(z, sin):
            b = work.tile([P, 4, D], F32, name="b", bufs=4)
            nc.vector.tensor_tensor(out=pairs(b[:]), in0=pairs(z)[:, :, :, ::-1], in1=pairs(sin), op=MULT)
            return b

        def rope_sum(engine, products, dst):
            y = work.tile([P, 4, D], F32, name="y", bufs=5)
            engine.tensor_tensor(out=y[:], in0=products[0][:], in1=products[1][:], op=ADD)
            nc.sync.dma_start(out=dst, in_=y[:])

        def token_project(c, j):
            acc = sum_bank()
            for g in range(PASSES):
                w, w_scale = weight(g, BANK * c, BANK * (c + 1))
                nc.tensor.matmul_mx(
                    out=acc[:],
                    lhsT=codes[g][:, P * j : P * (j + 1)].bitcast(E5M2X4),
                    lhsT_scale=scales[g][:, P * j : P * (j + 1)],
                    rhs=w,
                    rhs_scale=w_scale,
                    start=(g == 0),
                    stop=(g == PASSES - 1),
                )
            z = work.tile([P, CHUNK_HEADS, D], F32, name="z_token", bufs=3)
            nc.vector.tensor_tensor(out=z[:].rearrange("p h d -> p (h d)"), in0=acc[:], in1=bias_wide[:, c, :], op=ADD)
            return z

        def token_cos(z, j):
            return cos_product(z[:], table_ps[:, j : j + 1, 0:D].to_broadcast([P, CHUNK_HEADS, D]))

        def token_sin(z, j):
            return sin_product(z[:], table_ps[:, j : j + 1, D : 2 * D].to_broadcast([P, CHUNK_HEADS, D]))

        def token_products(z, j):
            return token_cos(z, j), token_sin(z, j)

        def token_out(c, j):
            heads = out_0[0, CHUNK_HEADS * c : CHUNK_HEADS * (c + 1)]
            return heads.rearrange("h (p j) d -> p h j d", j=TILES)[:, :, j, :]

        def feature_project(h):
            acc = sum_bank()
            for g in range(PASSES):
                w, w_scale = weight(g, D * h, D * (h + 1))
                nc.tensor.matmul_mx(
                    out=acc[:],
                    lhsT=w,
                    lhsT_scale=w_scale,
                    rhs=codes[g][:].bitcast(E5M2X4),
                    rhs_scale=scales[g][:],
                    start=(g == 0),
                    stop=(g == PASSES - 1),
                )
            z = work.tile([P, S], F32, name="z_feature", bufs=4)
            i = h - TOKEN_HEADS
            nc.scalar.activation(out=z[:], in_=acc[:], func=IDENTITY, bias=bias_col[:, i : i + 1])
            return z

        def feature_turn(h, z):
            turned = bank((6, 0, 1)[(h - TOKEN_HEADS) % 3])[:].rearrange("p (j d) -> p j d", d=D)
            for j in range(TILES):
                nc.tensor.transpose(turned[:, j, :], z[:, P * j : P * (j + 1)], ident[:])
            return turned

        def feature_products(turned):
            return cos_product(turned, table[:, :, 0:D]), sin_product(turned, table[:, :, D : 2 * D])

        def value_store(h, turned):
            y = work.tile([P, TILES, D], F32, name="y_value")
            nc.scalar.copy(out=y[:], in_=turned)
            nc.sync.dma_start(out=head_out(h), in_=y[:])

        transpose_x(0)
        quantize_x(0)
        spread_bias()
        table_to_psum()
        transpose_x(1)
        quantize_x(1)
        for j in range(2):
            z = token_project(0, j)
            transpose_x(j + 2)
            a = token_cos(z, j)
            quantize_x(j + 2)
            rope_sum(nc.gpsimd, (a, token_sin(z, j)), token_out(0, j))
        z2 = token_project(0, 2)
        z3 = token_project(0, 3)
        rope_sum(nc.gpsimd, token_products(z2, 2), token_out(0, 2))
        rope_sum(nc.gpsimd, token_products(z3, 3), token_out(0, 3))

        for j in range(TILES):
            first, second = TOKEN_HEADS + 2 * j, TOKEN_HEADS + 2 * j + 1
            z_first = feature_project(first)
            z_second = feature_project(second)
            z = token_project(1, j)
            turned_first = feature_turn(first, z_first)
            turned_second = feature_turn(second, z_second)
            rope_sum(nc.gpsimd, feature_products(turned_first), head_out(first))
            rope_sum(nc.gpsimd, token_products(z, j), token_out(1, j))
            rope_sum(nc.gpsimd, feature_products(turned_second), head_out(second))

        k0, k1, v0, v1 = range(H, HEADS)
        z_k0 = feature_project(k0)
        z_k1 = feature_project(k1)
        rope_sum(nc.gpsimd, feature_products(feature_turn(k0, z_k0)), head_out(k0))
        z_v0 = feature_project(v0)
        rope_sum(nc.vector, feature_products(feature_turn(k1, z_k1)), head_out(k1))
        z_v1 = feature_project(v1)
        value_store(v0, feature_turn(v0, z_v0))
        value_store(v1, feature_turn(v1, z_v1))
